import numpy as np
import ml_dtypes


def mxq(x, axis, fmt="e4m3"):
    dtype, down = {"e4m3": (ml_dtypes.float8_e4m3fn, 7), "e5m2": (ml_dtypes.float8_e5m2, 14)}[fmt]
    v = np.moveaxis(np.asarray(x, np.float32).astype(ml_dtypes.bfloat16).astype(np.float64), axis, -1)
    blocks = v.reshape(v.shape[:-1] + (-1, 32))
    amax = np.abs(blocks).max(-1, keepdims=True)
    byte = np.maximum(np.where(amax > 0, np.frexp(amax)[1] - 1 + 127, 0) - down, 1)
    scale = np.exp2(byte - 127.0)
    codes = (blocks / scale).astype(np.float32).astype(dtype).astype(np.float64)
    return np.moveaxis((codes * scale).reshape(v.shape), -1, axis)


WIDE = False


def mx_kscale(k):
    if not WIDE:
        return np.ones(k)
    levels = np.array([10, -10, 5, -5, 0])
    if k % 512:
        return np.exp2(np.random.permutation(np.resize(levels, k // 32))).repeat(32)
    a = np.empty((k // 512, 16))
    for p in range(k // 512):
        a[p, :8] = np.random.permutation(np.resize(levels, 8))
        for g in range(8):
            far = levels[np.abs(levels - a[p, g]) >= 10]
            a[p, g + 8] = far[np.random.randint(len(far))]
    return np.exp2(a.ravel()).repeat(32)


BF16 = ml_dtypes.bfloat16


def bf(x):
    return np.asarray(x, np.float32).astype(BF16)


def f64(x):
    return np.asarray(x).astype(np.float64)


B, T, D, DEPTH, F = 4, 1024, 1024, 4, 32
L = 2 ** DEPTH
N = L - 1
LF = L * F


def sigmoid(v):
    return 1.0 / (1.0 + np.exp(-v))


def leaf_probs(c):
    probs = np.ones(c.shape[:-1] + (1,))
    for m in range(DEPTH):
        start = 2 ** m - 1
        cl = c[..., start:start + 2 ** m]
        probs = np.stack([probs * cl, probs * (1.0 - cl)], axis=-1)
        probs = probs.reshape(probs.shape[:-2] + (-1,))
    return probs


def setup_inputs():
    s = mx_kscale(D)
    t = mx_kscale(LF).reshape(L, F)
    return {"x": bf(np.random.standard_normal((B, T, D)) * s),
            "node_logits": bf(np.random.standard_normal((B, T, N)) * 1.5),
            "node_b": bf(np.random.standard_normal(N) * 0.5),
            "w1": bf(np.random.standard_normal((L, D, F)) / np.sqrt(D) / s[None, :, None] * t[:, None, :]),
            "b1": bf(np.random.standard_normal((L, F)) * 0.5 * t),
            "w2": bf(np.random.standard_normal((L, F, D)) * 2.0 / np.sqrt(F) / t[:, :, None])}


def reference(x, node_logits, node_b, w1, b1, w2):
    probs = leaf_probs(sigmoid(f64(node_logits) + f64(node_b)))
    w1f = f64(w1).transpose(1, 0, 2).reshape(D, LF)
    a = mxq(f64(x), 2, "e4m3") @ mxq(w1f, 0, "e4m3")
    h = np.maximum(a.reshape(B, T, L, F) + f64(b1), 0.0) * probs[..., None]
    return mxq(h.reshape(B, T, LF), 2, "e4m3") @ mxq(f64(w2).reshape(LF, D), 0, "e4m3")

@@ -1,0 +1,308 @@
+from contextlib import ExitStack
+
+import concourse.mybir as mybir
+from concourse.masks import make_identity
+
+F32 = mybir.dt.float32
+BF16 = mybir.dt.bfloat16
+U32 = mybir.dt.uint32
+U8 = mybir.dt.uint8
+FP8X4 = mybir.dt.float8_e4m3fn_x4
+ALU = mybir.AluOpType
+ACT = mybir.ActivationFunctionType
+
+P = 128
+PACK = 4
+TOKENS = 4096
+D = 1024
+DEPTH = 4
+LEAVES = 16
+NODES = 15
+HIDDEN = 32
+LF = LEAVES * HIDDEN
+PASSES = D // (P * PACK)
+BANK = 512
+ROUND = 512
+ROUNDS = TOKENS // ROUND
+TILES = ROUND // P
+REPEAT = P // LEAVES
+X_BUFS = 6
+STEPS = ROUNDS * PACK
+LAG = 6
+AHEAD = 2
+X_PASSES = ROUNDS * PASSES
+W2_REGROUP_STEP = 1
+W2_QUANTISE_STEP = 3
+RUN = 4
+VECTOR_TILE = 1
+
+FLOPS = 2 * TOKENS * D * LF * 2
+
+
+def tile_fastfeedforwardnetwork_pa_t_kernel(tc, x, node_logits, node_b, w1, b1, w2, out):
+    nc = tc.nc
+    x_rounds = x.flatten_outer_dims().rearrange("(r p j) d -> r p (j d)", p=P, j=TILES)
+    out_rounds = out.flatten_outer_dims().rearrange("(r p j) e -> r p j e", p=P, j=TILES)
+
+    with ExitStack() as ctx:
+        keep = ctx.enter_context(tc.tile_pool(name="keep", bufs=1))
+        x_pool = ctx.enter_context(tc.tile_pool(name="x_pool", bufs=X_BUFS))
+        xg_pool = ctx.enter_context(tc.tile_pool(name="xg_pool", bufs=2))
+        xq_pool = ctx.enter_context(tc.tile_pool(name="xq_pool", bufs=3))
+        spread_pool = ctx.enter_context(tc.tile_pool(name="spread_pool", bufs=2))
+        h_pool = ctx.enter_context(tc.tile_pool(name="h_pool", bufs=2))
+        out_pool = ctx.enter_context(tc.tile_pool(name="out_pool", bufs=8))
+        a_psum = ctx.enter_context(tc.psum_pool(name="a_psum", bufs=3))
+        turn_psum = ctx.enter_context(tc.psum_pool(name="turn_psum", bufs=5))
+        ctx.enter_context(tc.manual_schedule())
+
+        x_tiles = {}
+
+        def load_x(r):
+            x_raw = x_pool.tile([P, TILES, D], BF16)
+            nc.sync.dma_start(out=x_raw[:].rearrange("p j d -> p (j d)"), in_=x_rounds[r])
+            x_tiles[r] = x_raw
+
+        logits = keep.tile([P, ROUNDS, TILES * NODES], BF16)
+        nc.sync.dma_start(
+            out=logits[:],
+            in_=node_logits.flatten_outer_dims().rearrange("(r p j) n -> p r (j n)", p=P, j=TILES),
+        )
+        node_bias = keep.tile([P, NODES], BF16)
+        nc.sync.dma_start(out=node_bias[:], in_=node_b.partition_broadcast(P))
+        b1_bf = keep.tile([P, PACK], BF16)
+        nc.sync.dma_start(out=b1_bf[:], in_=b1.rearrange("l (f s) -> (l f) s", s=PACK))
+        load_x(0)
+        w1_raw = keep.tile([P, LEAVES, PASSES, PACK, HIDDEN // PACK, PACK], BF16)
+        half_leaves = LEAVES // 2
+        for l0 in range(0, LEAVES, half_leaves):
+            nc.sync.dma_start(
+                out=w1_raw[:, l0 : l0 + half_leaves].rearrange("p l g t f s -> p (l g) (t f s)"),
+                in_=w1[l0 : l0 + half_leaves].rearrange("l (g p t) f -> p (l g) (t f)", p=P, t=PACK),
+            )
+        load_x(1)
+        w2_raw = keep.tile([P, PACK, D], BF16)
+        nc.sync.dma_start(
+            out=w2_raw[:].rearrange("p s e -> p (s e)"),
+            in_=w2.rearrange("l (f s) e -> (l f) (s e)", s=PACK),
+        )
+        for r in range(2, X_BUFS):
+            load_x(r)
+
+        ident = keep.tile([P, P], F32)
+        make_identity(nc, ident[:])
+
+        toks = ROUNDS * TILES
+        gate_in = keep.tile([P, toks, NODES], F32)
+        nc.vector.tensor_tensor(
+            out=gate_in[:],
+            in0=logits[:].rearrange("p r (j n) -> p (r j) n", n=NODES),
+            in1=node_bias[:].unsqueeze(1).to_broadcast([P, toks, NODES]),
+            op=ALU.add,
+        )
+        gates = keep.tile([P, toks, NODES, 2], F32)
+        nc.scalar.activation(out=gates[:, :, :, 0], in_=gate_in[:], func=ACT.Sigmoid)
+        nc.scalar.activation(out=gates[:, :, :, 1], in_=gate_in[:], func=ACT.Sigmoid, scale=-1.0)
+        probs = gates[:, :, 0, :]
+        for level in range(1, DEPTH):
+            nodes = 2 ** level
+            first = nodes - 1
+            children = keep.tile([P, toks, nodes, 2], F32, name="children%d" % level)
+            nc.vector.tensor_tensor(
+                out=children[:],
+                in0=probs.unsqueeze(3).to_broadcast([P, toks, nodes, 2]),
+                in1=gates[:, :, first : first + nodes, :],
+                op=ALU.mult,
+            )
+            probs = children[:].rearrange("p i n s -> p i (n s)")
+
+        b1_col = keep.tile([P, PACK], F32)
+        nc.vector.tensor_copy(out=b1_col[:], in_=b1_bf[:])
+
+        xg_tiles = {}
+        xq_tiles = {}
+
+        def transpose_x(r, g):
+            if g == 0:
+                x_grouped = xg_pool.tile([P, PASSES, ROUND, PACK], BF16, align_bytes=64)
+                x_codes = xq_pool.tile([P, PASSES, ROUND], U32, align_bytes=64)
+                x_scales = xq_pool.tile([P, PASSES, ROUND], U8, align_bytes=64)
+                xg_tiles[r] = x_grouped
+                xq_tiles[r] = (x_codes, x_scales)
+            x_words = x_tiles[r][:].bitcast(F32)
+            grouped_words = xg_tiles[r][:].bitcast(F32)
+            for half in range(2):
+                xt = turn_psum.tile([P, 2, 2 * P], F32, tag="turn")
+                for u in range(2):
+                    for jj in range(2):
+                        nc.tensor.transpose(
+                            xt[:, u, jj * P : (jj + 1) * P],
+                            x_words[:, 2 * half + jj, 2 * P * g + u : 2 * P * (g + 1) : 2],
+                            ident[:],
+                        )
+                nc.scalar.copy(
+                    out=grouped_words[:, g, half * 2 * P : (half + 1) * 2 * P, :],
+                    in_=xt[:].rearrange("p u w -> p w u"),
+                )
+
+        def quantise_x(r, g):
+            x_codes, x_scales = xq_tiles[r]
+            nc.vector.quantize_mx(
+                out=x_codes[:, g, :].bitcast(FP8X4),
+                scales=x_scales[:, g, :],
+                in_=xg_tiles[r][:, g].rearrange("p w t -> p (w t)"),
+            )
+
+        leaf_rows = keep.tile([P, ROUNDS, ROUND], F32)
+
+        def spread_probs(r):
+            spread = spread_pool.tile([P, TILES, LEAVES, REPEAT], F32)
+            nc.vector.tensor_copy(
+                out=spread[:],
+                in_=probs[:, r * TILES : (r + 1) * TILES, :].unsqueeze(3).to_broadcast([P, TILES, LEAVES, REPEAT]),
+            )
+            rows = turn_psum.tile([P, BANK], F32, tag="turn")
+            for j in range(TILES):
+                nc.tensor.transpose(
+                    rows[:, j * P : (j + 1) * P], spread[:, j].rearrange("p l c -> p (l c)"), ident[:]
+                )
+            nc.scalar.copy(out=leaf_rows[:, r, :], in_=rows[:])
+
+        w1_codes = keep.tile([P, PASSES, PACK, P], U32, align_bytes=64)
+        w1_scales = keep.tile([P, PASSES, PACK, P], U8, align_bytes=64)
+        w2_codes = keep.tile([P, D], U32, align_bytes=64)
+        w2_scales = keep.tile([P, D], U8, align_bytes=64)
+        w2_grouped = keep.tile([P, D, PACK], BF16, align_bytes=64)
+
+        def prepare_w1():
+            w1_grouped = keep.tile([P, PASSES, PACK, P, PACK], BF16, align_bytes=64)
+            for l0 in range(0, LEAVES, half_leaves):
+                for g in range(PASSES):
+                    for s in range(PACK):
+                        nc.vector.tensor_copy(
+                            out=w1_grouped[:, g, s, l0 * REPEAT : (l0 + half_leaves) * REPEAT, :].rearrange(
+                                "p (l f) t -> p l f t", l=half_leaves
+                            ),
+                            in_=w1_raw[:, l0 : l0 + half_leaves, g, :, :, s].rearrange("p l t f -> p l f t"),
+                        )
+            nc.vector.quantize_mx(
+                out=w1_codes[:].rearrange("p g s m -> p (g s m)").bitcast(FP8X4),
+                scales=w1_scales[:].rearrange("p g s m -> p (g s m)"),
+                in_=w1_grouped[:].rearrange("p g s m t -> p (g s m t)"),
+            )
+
+        def regroup_w2():
+            nc.vector.tensor_copy(
+                out=w2_grouped[:, 0:BANK, :], in_=w2_raw[:, :, 0:BANK].rearrange("p s e -> p e s")
+            )
+            nc.scalar.copy(out=w2_grouped[:, BANK:D, :], in_=w2_raw[:, :, BANK:D].rearrange("p s e -> p e s"))
+
+        def quantise_w2():
+            nc.vector.quantize_mx(
+                out=w2_codes[:].bitcast(FP8X4),
+                scales=w2_scales[:],
+                in_=w2_grouped[:].rearrange("p e s -> p (e s)"),
+            )
+
+        weighted_tiles = {}
+        h_grouped_tiles = {}
+        hq_tiles = {}
+
+        def hidden_sums(r, s):
+            if s == 0:
+                weighted = h_pool.tile([P, PACK, ROUND], BF16)
+                weighted_tiles[r] = weighted
+            x_codes, x_scales = xq_tiles[r]
+            a = a_psum.tile([P, BANK], F32)
+            for g in range(PASSES):
+                nc.tensor.matmul_mx(
+                    out=a[:],
+                    lhsT=w1_codes[:, g, s, :].bitcast(FP8X4),
+                    lhsT_scale=w1_scales[:, g, s, :],
+                    rhs=x_codes[:, g, :].bitcast(FP8X4),
+                    rhs_scale=x_scales[:, g, :],
+                    start=(g == 0),
+                    stop=(g == PASSES - 1),
+                )
+            nc.vector.scalar_tensor_tensor(
+                out=weighted_tiles[r][:, s, :],
+                in0=a[:],
+                scalar=b1_col[:, s : s + 1],
+                in1=leaf_rows[:, r, :],
+                op0=ALU.add,
+                op1=ALU.mult,
+            )
+
+        def relu_hidden(r):
+            h_grouped = h_pool.tile([P, ROUND, PACK], BF16, align_bytes=64)
+            nc.vector.tensor_scalar(
+                out=h_grouped[:].rearrange("p (c i) s -> p c s i", i=RUN),
+                in0=weighted_tiles[r][:].rearrange("p s (c i) -> p c s i", i=RUN),
+                scalar1=0.0,
+                scalar2=None,
+                op0=ALU.max,
+            )
+            h_grouped_tiles[r] = h_grouped
+
+        def quantise_hidden(r):
+            h_codes = h_pool.tile([P, ROUND], U32, align_bytes=64)
+            h_scales = h_pool.tile([P, ROUND], U8, align_bytes=64)
+            nc.vector.quantize_mx(
+                out=h_codes[:].bitcast(FP8X4),
+                scales=h_scales[:],
+                in_=h_grouped_tiles[r][:].rearrange("p w s -> p (w s)"),
+            )
+            hq_tiles[r] = (h_codes, h_scales)
+
+        def output_tile(r, j):
+            h_codes, h_scales = hq_tiles[r]
+            result = out_pool.tile([P, D], F32)
+            for half in range(D // BANK):
+                e0 = half * BANK
+                o = turn_psum.tile([P, BANK], F32, tag="turn")
+                nc.tensor.matmul_mx(
+                    out=o[:],
+                    lhsT=h_codes[:, j * P : (j + 1) * P].bitcast(FP8X4),
+                    lhsT_scale=h_scales[:, j * P : (j + 1) * P],
+                    rhs=w2_codes[:, e0 : e0 + BANK].bitcast(FP8X4),
+                    rhs_scale=w2_scales[:, e0 : e0 + BANK],
+                    start=True,
+                    stop=True,
+                )
+                if half == 1 and (j == VECTOR_TILE or r == ROUNDS - 1):
+                    nc.vector.tensor_copy(out=result[:, e0 : e0 + BANK], in_=o[:])
+                else:
+                    nc.scalar.copy(out=result[:, e0 : e0 + BANK], in_=o[:])
+            nc.sync.dma_start(out=out_rounds[r][:, j, :], in_=result[:])
+
+        for g in range(PASSES):
+            transpose_x(0, g)
+        load_x(X_BUFS)
+        for r in range(ROUNDS):
+            spread_probs(r)
+        for g in range(PASSES):
+            quantise_x(0, g)
+        prepare_w1()
+        for g in range(PASSES):
+            transpose_x(1, g)
+        load_x(X_BUFS + 1)
+        for g in range(PASSES):
+            quantise_x(1, g)
+        for step in range(STEPS + LAG):
+            r, s = divmod(step, PACK)
+            if step < STEPS:
+                hidden_sums(r, s)
+            if step == W2_REGROUP_STEP:
+                regroup_w2()
+            if step == W2_QUANTISE_STEP:
+                quantise_w2()
+            x_pass = step // 2 + AHEAD * PASSES
+            if step % 2 == 0 and step > 0 and x_pass - 1 < X_PASSES:
+                quantise_x(*divmod(x_pass - 1, PASSES))
+            if step >= LAG:
+                output_tile(*divmod(step - LAG, TILES))
+            if step % 2 == 1 and x_pass < X_PASSES:
+                transpose_x(*divmod(x_pass, PASSES))
+            if step < STEPS and s == PACK - 1:
+                relu_hidden(r)
+                quantise_hidden(r)

@@ -22,17 +22,16 @@ HIDDEN = 32
 LF = LEAVES * HIDDEN
 PASSES = D // (P * PACK)
 BANK = 512
+REPEAT = P // LEAVES
+X_BUFS = 6
 ROUND = 512
 ROUNDS = TOKENS // ROUND
 TILES = ROUND // P
-REPEAT = P // LEAVES
-X_BUFS = 6
-STEPS = ROUNDS * PACK
-LAG = 6
-AHEAD = 2
-X_PASSES = ROUNDS * PASSES
-W2_REGROUP_STEP = 1
-W2_QUANTISE_STEP = 3
+CHUNK_TILES = (2, 2, 4, 4, 4, 4, 4, 4, 2, 2)
+CHUNKS = len(CHUNK_TILES)
+FIRST_TILE = tuple(sum(CHUNK_TILES[:c]) for c in range(CHUNKS))
+OUT_LAG = 2
+X_LEAD = (5, 3)
 RUN = 4
 VECTOR_TILE = 1
 
@@ -41,7 +40,7 @@ FLOPS = 2 * TOKENS * D * LF * 2
 
 def tile_fastfeedforwardnetwork_pa_t_kernel(tc, x, node_logits, node_b, w1, b1, w2, out):
     nc = tc.nc
-    x_rounds = x.flatten_outer_dims().rearrange("(r p j) d -> r p (j d)", p=P, j=TILES)
+    x_rounds = x.flatten_outer_dims().rearrange("(r p j) d -> r p j d", p=P, j=TILES)
     out_rounds = out.flatten_outer_dims().rearrange("(r p j) e -> r p j e", p=P, j=TILES)
 
     with ExitStack() as ctx:
@@ -56,54 +55,62 @@ def tile_fastfeedforwardnetwork_pa_t_kernel(tc, x, node_logits, node_b, w1, b1, 
         turn_psum = ctx.enter_context(tc.psum_pool(name="turn_psum", bufs=5))
         ctx.enter_context(tc.manual_schedule())
 
-        x_tiles = {}
-
-        def load_x(r):
-            x_raw = x_pool.tile([P, TILES, D], BF16)
-            nc.sync.dma_start(out=x_raw[:].rearrange("p j d -> p (j d)"), in_=x_rounds[r])
-            x_tiles[r] = x_raw
-
-        logits = keep.tile([P, ROUNDS, TILES * NODES], BF16)
-        nc.sync.dma_start(
-            out=logits[:],
+        toks = TOKENS // P
+        logits = keep.tile([P, toks, NODES], BF16)
+        nc.scalar.dma_start(
+            out=logits[:].rearrange("p (r j) n -> p r (j n)", j=TILES),
             in_=node_logits.flatten_outer_dims().rearrange("(r p j) n -> p r (j n)", p=P, j=TILES),
         )
         node_bias = keep.tile([P, NODES], BF16)
-        nc.sync.dma_start(out=node_bias[:], in_=node_b.partition_broadcast(P))
+        nc.scalar.dma_start(out=node_bias[:], in_=node_b.partition_broadcast(P))
         b1_bf = keep.tile([P, PACK], BF16)
-        nc.sync.dma_start(out=b1_bf[:], in_=b1.rearrange("l (f s) -> (l f) s", s=PACK))
-        load_x(0)
-        w1_raw = keep.tile([P, LEAVES, PASSES, PACK, HIDDEN // PACK, PACK], BF16)
-        half_leaves = LEAVES // 2
-        for l0 in range(0, LEAVES, half_leaves):
+        nc.scalar.dma_start(out=b1_bf[:], in_=b1.rearrange("l (f s) -> (l f) s", s=PACK))
+
+        x_tiles = {}
+
+        def load_x(r, j0=0, j1=TILES):
+            if j0 == 0:
+                x_raw = x_pool.tile([P, TILES, D], BF16)
+                x_tiles[r] = x_raw
+            nc.sync.dma_start(out=x_tiles[r][:, j0:j1], in_=x_rounds[r][:, j0:j1])
+
+        load_x(0, 0, TILES // 2)
+        w1_raw = keep.tile([P, PASSES, LEAVES, PACK, HIDDEN // PACK, PACK], BF16)
+        for g in range(PASSES):
             nc.sync.dma_start(
-                out=w1_raw[:, l0 : l0 + half_leaves].rearrange("p l g t f s -> p (l g) (t f s)"),
-                in_=w1[l0 : l0 + half_leaves].rearrange("l (g p t) f -> p (l g) (t f)", p=P, t=PACK),
+                out=w1_raw[:, g].rearrange("p l t f s -> p l (t f s)"),
+                in_=w1[:, g * P * PACK : (g + 1) * P * PACK, :].rearrange("l (p t) f -> p l (t f)", p=P, t=PACK),
             )
-        load_x(1)
+        load_x(0, TILES // 2, TILES)
         w2_raw = keep.tile([P, PACK, D], BF16)
         nc.sync.dma_start(
             out=w2_raw[:].rearrange("p s e -> p (s e)"),
             in_=w2.rearrange("l (f s) e -> (l f) (s e)", s=PACK),
         )
-        for r in range(2, X_BUFS):
+        for r in range(1, X_BUFS):
             load_x(r)
+
+        warm = keep.tile([P, 1], F32)
+        nc.gpsimd.memset(warm[:], 0.0)
+        nc.scalar.activation(out=warm[:], in_=warm[:], func=ACT.Sigmoid)
 
         ident = keep.tile([P, P], F32)
         make_identity(nc, ident[:])
 
-        toks = ROUNDS * TILES
         gate_in = keep.tile([P, toks, NODES], F32)
         nc.vector.tensor_tensor(
             out=gate_in[:],
-            in0=logits[:].rearrange("p r (j n) -> p (r j) n", n=NODES),
+            in0=logits[:],
             in1=node_bias[:].unsqueeze(1).to_broadcast([P, toks, NODES]),
             op=ALU.add,
         )
-        gates = keep.tile([P, toks, NODES, 2], F32)
-        nc.scalar.activation(out=gates[:, :, :, 0], in_=gate_in[:], func=ACT.Sigmoid)
-        nc.scalar.activation(out=gates[:, :, :, 1], in_=gate_in[:], func=ACT.Sigmoid, scale=-1.0)
-        probs = gates[:, :, 0, :]
+        b1_col = keep.tile([P, PACK], F32)
+        nc.vector.tensor_copy(out=b1_col[:], in_=b1_bf[:])
+        gates = keep.tile([P, 2, toks, NODES], F32)
+        nc.scalar.activation(out=gates[:, 0], in_=gate_in[:], func=ACT.Sigmoid)
+        nc.scalar.activation(out=gates[:, 1], in_=gate_in[:], func=ACT.Sigmoid, scale=-1.0)
+        sides = gates[:].rearrange("p s i n -> p i n s")
+        probs = sides[:, :, 0, :]
         for level in range(1, DEPTH):
             nodes = 2 ** level
             first = nodes - 1
@@ -111,33 +118,32 @@ def tile_fastfeedforwardnetwork_pa_t_kernel(tc, x, node_logits, node_b, w1, b1, 
             nc.vector.tensor_tensor(
                 out=children[:],
                 in0=probs.unsqueeze(3).to_broadcast([P, toks, nodes, 2]),
-                in1=gates[:, :, first : first + nodes, :],
+                in1=sides[:, :, first : first + nodes, :],
                 op=ALU.mult,
             )
             probs = children[:].rearrange("p i n s -> p i (n s)")
 
-        b1_col = keep.tile([P, PACK], F32)
-        nc.vector.tensor_copy(out=b1_col[:], in_=b1_bf[:])
-
         xg_tiles = {}
         xq_tiles = {}
 
-        def transpose_x(r, g):
+        def transpose_x(c, g):
+            tiles = CHUNK_TILES[c]
             if g == 0:
-                x_grouped = xg_pool.tile([P, PASSES, ROUND, PACK], BF16, align_bytes=64)
-                x_codes = xq_pool.tile([P, PASSES, ROUND], U32, align_bytes=64)
-                x_scales = xq_pool.tile([P, PASSES, ROUND], U8, align_bytes=64)
-                xg_tiles[r] = x_grouped
-                xq_tiles[r] = (x_codes, x_scales)
+                x_grouped = xg_pool.tile([P, PASSES, tiles * P, PACK], BF16, align_bytes=64)
+                x_codes = xq_pool.tile([P, PASSES, tiles * P], U32, align_bytes=64)
+                x_scales = xq_pool.tile([P, PASSES, tiles * P], U8, align_bytes=64)
+                xg_tiles[c] = x_grouped
+                xq_tiles[c] = (x_codes, x_scales)
+            r, j0 = divmod(FIRST_TILE[c], TILES)
             x_words = x_tiles[r][:].bitcast(F32)
-            grouped_words = xg_tiles[r][:].bitcast(F32)
-            for half in range(2):
+            grouped_words = xg_tiles[c][:].bitcast(F32)
+            for half in range(tiles // 2):
                 xt = turn_psum.tile([P, 2, 2 * P], F32, tag="turn")
                 for u in range(2):
                     for jj in range(2):
                         nc.tensor.transpose(
                             xt[:, u, jj * P : (jj + 1) * P],
-                            x_words[:, 2 * half + jj, 2 * P * g + u : 2 * P * (g + 1) : 2],
+                            x_words[:, j0 + 2 * half + jj, 2 * P * g + u : 2 * P * (g + 1) : 2],
                             ident[:],
                         )
                 nc.scalar.copy(
@@ -145,75 +151,93 @@ def tile_fastfeedforwardnetwork_pa_t_kernel(tc, x, node_logits, node_b, w1, b1, 
                     in_=xt[:].rearrange("p u w -> p w u"),
                 )
 
-        def quantise_x(r, g):
-            x_codes, x_scales = xq_tiles[r]
+        def quantise_x(c, g):
+            x_codes, x_scales = xq_tiles[c]
             nc.vector.quantize_mx(
                 out=x_codes[:, g, :].bitcast(FP8X4),
                 scales=x_scales[:, g, :],
-                in_=xg_tiles[r][:, g].rearrange("p w t -> p (w t)"),
+                in_=xg_tiles[c][:, g].rearrange("p w t -> p (w t)"),
             )
 
-        leaf_rows = keep.tile([P, ROUNDS, ROUND], F32)
+        leaf_rows = keep.tile([P, TOKENS], F32)
 
-        def spread_probs(r):
-            spread = spread_pool.tile([P, TILES, LEAVES, REPEAT], F32)
+        def columns_of(c):
+            return slice(FIRST_TILE[c] * P, (FIRST_TILE[c] + CHUNK_TILES[c]) * P)
+
+        spread_tiles = {}
+
+        def spread_probs(c):
+            tiles = CHUNK_TILES[c]
+            i0 = FIRST_TILE[c]
+            spread = spread_pool.tile([P, tiles, LEAVES, REPEAT], F32)
             nc.vector.tensor_copy(
                 out=spread[:],
-                in_=probs[:, r * TILES : (r + 1) * TILES, :].unsqueeze(3).to_broadcast([P, TILES, LEAVES, REPEAT]),
+                in_=probs[:, i0 : i0 + tiles, :].unsqueeze(3).to_broadcast([P, tiles, LEAVES, REPEAT]),
             )
-            rows = turn_psum.tile([P, BANK], F32, tag="turn")
-            for j in range(TILES):
+            spread_tiles[c] = spread
+
+        def turn_probs(c):
+            tiles = CHUNK_TILES[c]
+            spread = spread_tiles[c]
+            rows = turn_psum.tile([P, tiles * P], F32, tag="turn")
+            for j in range(tiles):
                 nc.tensor.transpose(
                     rows[:, j * P : (j + 1) * P], spread[:, j].rearrange("p l c -> p (l c)"), ident[:]
                 )
-            nc.scalar.copy(out=leaf_rows[:, r, :], in_=rows[:])
+            nc.scalar.copy(out=leaf_rows[:, columns_of(c)], in_=rows[:])
 
+        w1_grouped = keep.tile([P, PASSES, PACK, P, PACK], BF16, align_bytes=64)
         w1_codes = keep.tile([P, PASSES, PACK, P], U32, align_bytes=64)
         w1_scales = keep.tile([P, PASSES, PACK, P], U8, align_bytes=64)
         w2_codes = keep.tile([P, D], U32, align_bytes=64)
         w2_scales = keep.tile([P, D], U8, align_bytes=64)
         w2_grouped = keep.tile([P, D, PACK], BF16, align_bytes=64)
 
-        def prepare_w1():
-            w1_grouped = keep.tile([P, PASSES, PACK, P, PACK], BF16, align_bytes=64)
-            for l0 in range(0, LEAVES, half_leaves):
-                for g in range(PASSES):
-                    for s in range(PACK):
-                        nc.vector.tensor_copy(
-                            out=w1_grouped[:, g, s, l0 * REPEAT : (l0 + half_leaves) * REPEAT, :].rearrange(
-                                "p (l f) t -> p l f t", l=half_leaves
-                            ),
-                            in_=w1_raw[:, l0 : l0 + half_leaves, g, :, :, s].rearrange("p l t f -> p l f t"),
-                        )
+        def regroup_w1(copy, g, s):
+            copy(
+                out=w1_grouped[:, g, s].rearrange("p (l f) t -> p l f t", l=LEAVES),
+                in_=w1_raw[:, g, :, :, :, s].rearrange("p l t f -> p l f t"),
+            )
+
+        def quantise_w1(g, s0, s1):
             nc.vector.quantize_mx(
-                out=w1_codes[:].rearrange("p g s m -> p (g s m)").bitcast(FP8X4),
-                scales=w1_scales[:].rearrange("p g s m -> p (g s m)"),
-                in_=w1_grouped[:].rearrange("p g s m t -> p (g s m t)"),
+                out=w1_codes[:, g, s0:s1].rearrange("p s m -> p (s m)").bitcast(FP8X4),
+                scales=w1_scales[:, g, s0:s1].rearrange("p s m -> p (s m)"),
+                in_=w1_grouped[:, g, s0:s1].rearrange("p s m t -> p (s m t)"),
             )
 
         def regroup_w2():
             nc.vector.tensor_copy(
-                out=w2_grouped[:, 0:BANK, :], in_=w2_raw[:, :, 0:BANK].rearrange("p s e -> p e s")
+                out=w2_grouped[:, 0:BANK, :].rearrange("p (c i) s -> p c s i", i=RUN),
+                in_=w2_raw[:, :, 0:BANK].rearrange("p s (c i) -> p c s i", i=RUN),
             )
-            nc.scalar.copy(out=w2_grouped[:, BANK:D, :], in_=w2_raw[:, :, BANK:D].rearrange("p s e -> p e s"))
+            nc.gpsimd.tensor_scalar(
+                out=w2_grouped[:, BANK:D, :],
+                in0=w2_raw[:, :, BANK:D].rearrange("p s e -> p e s"),
+                scalar1=1.0,
+                scalar2=0.0,
+                op0=ALU.mult,
+                op1=ALU.add,
+            )
 
-        def quantise_w2():
+        def quantise_w2(e0, e1):
             nc.vector.quantize_mx(
-                out=w2_codes[:].bitcast(FP8X4),
-                scales=w2_scales[:],
-                in_=w2_grouped[:].rearrange("p e s -> p (e s)"),
+                out=w2_codes[:, e0:e1].bitcast(FP8X4),
+                scales=w2_scales[:, e0:e1],
+                in_=w2_grouped[:, e0:e1].rearrange("p e s -> p (e s)"),
             )
 
         weighted_tiles = {}
         h_grouped_tiles = {}
         hq_tiles = {}
 
-        def hidden_sums(r, s):
+        def hidden_sums(c, s):
+            tokens = CHUNK_TILES[c] * P
             if s == 0:
-                weighted = h_pool.tile([P, PACK, ROUND], BF16)
-                weighted_tiles[r] = weighted
-            x_codes, x_scales = xq_tiles[r]
-            a = a_psum.tile([P, BANK], F32)
+                weighted = h_pool.tile([P, PACK, tokens], BF16)
+                weighted_tiles[c] = weighted
+            x_codes, x_scales = xq_tiles[c]
+            a = a_psum.tile([P, tokens], F32)
             for g in range(PASSES):
                 nc.tensor.matmul_mx(
                     out=a[:],
@@ -225,37 +249,38 @@ def tile_fastfeedforwardnetwork_pa_t_kernel(tc, x, node_logits, node_b, w1, b1, 
                     stop=(g == PASSES - 1),
                 )
             nc.vector.scalar_tensor_tensor(
-                out=weighted_tiles[r][:, s, :],
+                out=weighted_tiles[c][:, s, :],
                 in0=a[:],
                 scalar=b1_col[:, s : s + 1],
-                in1=leaf_rows[:, r, :],
+                in1=leaf_rows[:, columns_of(c)],
                 op0=ALU.add,
                 op1=ALU.mult,
             )
 
-        def relu_hidden(r):
-            h_grouped = h_pool.tile([P, ROUND, PACK], BF16, align_bytes=64)
+        def relu_hidden(c):
+            h_grouped = h_pool.tile([P, CHUNK_TILES[c] * P, PACK], BF16, align_bytes=64)
             nc.vector.tensor_scalar(
                 out=h_grouped[:].rearrange("p (c i) s -> p c s i", i=RUN),
-                in0=weighted_tiles[r][:].rearrange("p s (c i) -> p c s i", i=RUN),
+                in0=weighted_tiles[c][:].rearrange("p s (c i) -> p c s i", i=RUN),
                 scalar1=0.0,
                 scalar2=None,
                 op0=ALU.max,
             )
-            h_grouped_tiles[r] = h_grouped
+            h_grouped_tiles[c] = h_grouped
 
-        def quantise_hidden(r):
-            h_codes = h_pool.tile([P, ROUND], U32, align_bytes=64)
-            h_scales = h_pool.tile([P, ROUND], U8, align_bytes=64)
+        def quantise_hidden(c):
+            tokens = CHUNK_TILES[c] * P
+            h_codes = h_pool.tile([P, tokens], U32, align_bytes=64)
+            h_scales = h_pool.tile([P, tokens], U8, align_bytes=64)
             nc.vector.quantize_mx(
                 out=h_codes[:].bitcast(FP8X4),
                 scales=h_scales[:],
-                in_=h_grouped_tiles[r][:].rearrange("p w s -> p (w s)"),
+                in_=h_grouped_tiles[c][:].rearrange("p w s -> p (w s)"),
             )
-            hq_tiles[r] = (h_codes, h_scales)
+            hq_tiles[c] = (h_codes, h_scales)
 
-        def output_tile(r, j):
-            h_codes, h_scales = hq_tiles[r]
+        def output_tile(c, j):
+            h_codes, h_scales = hq_tiles[c]
             result = out_pool.tile([P, D], F32)
             for half in range(D // BANK):
                 e0 = half * BANK
@@ -269,40 +294,78 @@ def tile_fastfeedforwardnetwork_pa_t_kernel(tc, x, node_logits, node_b, w1, b1, 
                     start=True,
                     stop=True,
                 )
-                if half == 1 and (j == VECTOR_TILE or r == ROUNDS - 1):
+                if half == 1 and ((FIRST_TILE[c] + j) % TILES == VECTOR_TILE or c >= CHUNKS - 2):
                     nc.vector.tensor_copy(out=result[:, e0 : e0 + BANK], in_=o[:])
                 else:
                     nc.scalar.copy(out=result[:, e0 : e0 + BANK], in_=o[:])
-            nc.sync.dma_start(out=out_rounds[r][:, j, :], in_=result[:])
+            nc.sync.dma_start(
+                out=out_rounds[(FIRST_TILE[c] + j) // TILES][:, (FIRST_TILE[c] + j) % TILES, :],
+                in_=result[:],
+            )
 
         for g in range(PASSES):
             transpose_x(0, g)
-        load_x(X_BUFS)
-        for r in range(ROUNDS):
-            spread_probs(r)
+        for c in range(2):
+            spread_probs(c)
+            turn_probs(c)
         for g in range(PASSES):
             quantise_x(0, g)
-        prepare_w1()
+        spread_probs(2)
+        turn_probs(2)
+        for s in range(PACK):
+            regroup_w1(nc.vector.tensor_copy, 0, s)
+        quantise_w1(0, 0, PACK)
+        for s in range(2, PACK):
+            regroup_w1(nc.scalar.copy, 1, s)
+        for s in range(2):
+            regroup_w1(nc.vector.tensor_copy, 1, s)
+            quantise_w1(1, s, s + 1)
         for g in range(PASSES):
             transpose_x(1, g)
-        load_x(X_BUFS + 1)
-        for g in range(PASSES):
-            quantise_x(1, g)
-        for step in range(STEPS + LAG):
-            r, s = divmod(step, PACK)
-            if step < STEPS:
-                hidden_sums(r, s)
-            if step == W2_REGROUP_STEP:
-                regroup_w2()
-            if step == W2_QUANTISE_STEP:
-                quantise_w2()
-            x_pass = step // 2 + AHEAD * PASSES
-            if step % 2 == 0 and step > 0 and x_pass - 1 < X_PASSES:
-                quantise_x(*divmod(x_pass - 1, PASSES))
-            if step >= LAG:
-                output_tile(*divmod(step - LAG, TILES))
-            if step % 2 == 1 and x_pass < X_PASSES:
-                transpose_x(*divmod(x_pass, PASSES))
-            if step < STEPS and s == PACK - 1:
-                relu_hidden(r)
-                quantise_hidden(r)
+
+        x_due = [(2, 2, 0), (3, 2, 1)] + [
+            (FIRST_TILE[c] - X_LEAD[g if CHUNK_TILES[c] == TILES else 1], c, g)
+            for c in range(3, CHUNKS)
+            for g in range(PASSES)
+        ]
+        out_due = [
+            (FIRST_TILE[c] + CHUNK_TILES[c] + OUT_LAG + j, c, j) for c in range(CHUNKS) for j in range(CHUNK_TILES[c])
+        ]
+        to_quantise = [(1, 0), (1, 1)]
+        to_spread = list(range(3, CHUNKS))
+        to_turn = []
+        to_load = list(range(X_BUFS, ROUNDS))
+        for c in range(CHUNKS):
+            for s in range(PACK):
+                clock = FIRST_TILE[c] + s * CHUNK_TILES[c] / PACK
+                hidden_sums(c, s)
+                if c == 0 and s in (0, 1):
+                    quantise_w1(1, s + 2, s + 3)
+                while to_quantise:
+                    quantise_x(*to_quantise.pop(0))
+                if c == 0 and s == 2:
+                    regroup_w2()
+                if c == 0 and s == 3:
+                    quantise_w2(0, BANK)
+                if c == 1 and s == 0:
+                    quantise_w2(BANK, D)
+                while out_due and out_due[0][0] <= clock:
+                    output_tile(*out_due.pop(0)[1:])
+                if s == PACK - 1:
+                    relu_hidden(c)
+                if x_due and x_due[0][0] <= clock:
+                    if to_turn:
+                        turn_probs(to_turn.pop(0))
+                    while x_due and x_due[0][0] <= clock:
+                        due, xc, g = x_due.pop(0)
+                        transpose_x(xc, g)
+                        to_quantise.append((xc, g))
+                        if g == PASSES - 1 and CHUNK_TILES[xc] == TILES and to_load:
+                            load_x(to_load.pop(0))
+                if s == PACK - 1:
+                    quantise_hidden(c)
+                if to_spread and not to_turn:
+                    to_turn.append(to_spread[0])
+                    spread_probs(to_spread.pop(0))
+        for due, c, j in out_due:
+            output_tile(c, j)

@@ -27,13 +27,17 @@ X_BUFS = 6
 ROUND = 512
 ROUNDS = TOKENS // ROUND
 TILES = ROUND // P
-CHUNK_TILES = (2, 2, 4, 4, 4, 4, 4, 4, 2, 2)
+CHUNK_TILES = (4, 4, 4, 4, 4, 4, 4, 2, 2)
 CHUNKS = len(CHUNK_TILES)
 FIRST_TILE = tuple(sum(CHUNK_TILES[:c]) for c in range(CHUNKS))
 OUT_LAG = 2
-X_LEAD = (5, 3)
+X_DUE = lambda k: k if k < 6 else 2 * k - 5
+W2_STEP = 2
+SPREAD_HEAD = 5
+SPREAD_STEP = 1
+VSHARE = (1,)
+VFROM = 28
 RUN = 4
-VECTOR_TILE = 1
 
 FLOPS = 2 * TOKENS * D * LF * 2
 
@@ -47,8 +51,8 @@ def tile_fastfeedforwardnetwork_pa_t_kernel(tc, x, node_logits, node_b, w1, b1, 
         keep = ctx.enter_context(tc.tile_pool(name="keep", bufs=1))
         x_pool = ctx.enter_context(tc.tile_pool(name="x_pool", bufs=X_BUFS))
         xg_pool = ctx.enter_context(tc.tile_pool(name="xg_pool", bufs=2))
-        xq_pool = ctx.enter_context(tc.tile_pool(name="xq_pool", bufs=3))
-        spread_pool = ctx.enter_context(tc.tile_pool(name="spread_pool", bufs=2))
+        xq_pool = ctx.enter_context(tc.tile_pool(name="xq_pool", bufs=4))
+        spread_pool = ctx.enter_context(tc.tile_pool(name="spread_pool", bufs=8))
         h_pool = ctx.enter_context(tc.tile_pool(name="h_pool", bufs=2))
         out_pool = ctx.enter_context(tc.tile_pool(name="out_pool", bufs=8))
         a_psum = ctx.enter_context(tc.psum_pool(name="a_psum", bufs=3))
@@ -57,14 +61,12 @@ def tile_fastfeedforwardnetwork_pa_t_kernel(tc, x, node_logits, node_b, w1, b1, 
 
         toks = TOKENS // P
         logits = keep.tile([P, toks, NODES], BF16)
-        nc.scalar.dma_start(
+        nc.sync.dma_start(
             out=logits[:].rearrange("p (r j) n -> p r (j n)", j=TILES),
             in_=node_logits.flatten_outer_dims().rearrange("(r p j) n -> p r (j n)", p=P, j=TILES),
         )
         node_bias = keep.tile([P, NODES], BF16)
-        nc.scalar.dma_start(out=node_bias[:], in_=node_b.partition_broadcast(P))
-        b1_bf = keep.tile([P, PACK], BF16)
-        nc.scalar.dma_start(out=b1_bf[:], in_=b1.rearrange("l (f s) -> (l f) s", s=PACK))
+        nc.sync.dma_start(out=node_bias[:], in_=node_b.partition_broadcast(P))
 
         x_tiles = {}
 
@@ -75,19 +77,22 @@ def tile_fastfeedforwardnetwork_pa_t_kernel(tc, x, node_logits, node_b, w1, b1, 
             nc.sync.dma_start(out=x_tiles[r][:, j0:j1], in_=x_rounds[r][:, j0:j1])
 
         load_x(0, 0, TILES // 2)
+        load_x(0, TILES // 2, TILES)
         w1_raw = keep.tile([P, PASSES, LEAVES, PACK, HIDDEN // PACK, PACK], BF16)
         for g in range(PASSES):
             nc.sync.dma_start(
                 out=w1_raw[:, g].rearrange("p l t f s -> p l (t f s)"),
                 in_=w1[:, g * P * PACK : (g + 1) * P * PACK, :].rearrange("l (p t) f -> p l (t f)", p=P, t=PACK),
             )
-        load_x(0, TILES // 2, TILES)
+        b1_bf = keep.tile([P, PACK], BF16)
+        nc.sync.dma_start(out=b1_bf[:], in_=b1.rearrange("l (f s) -> (l f) s", s=PACK))
+        load_x(1)
         w2_raw = keep.tile([P, PACK, D], BF16)
         nc.sync.dma_start(
             out=w2_raw[:].rearrange("p s e -> p (s e)"),
             in_=w2.rearrange("l (f s) e -> (l f) (s e)", s=PACK),
         )
-        for r in range(1, X_BUFS):
+        for r in range(2, X_BUFS):
             load_x(r)
 
         warm = keep.tile([P, 1], F32)
@@ -104,8 +109,6 @@ def tile_fastfeedforwardnetwork_pa_t_kernel(tc, x, node_logits, node_b, w1, b1, 
             in1=node_bias[:].unsqueeze(1).to_broadcast([P, toks, NODES]),
             op=ALU.add,
         )
-        b1_col = keep.tile([P, PACK], F32)
-        nc.vector.tensor_copy(out=b1_col[:], in_=b1_bf[:])
         gates = keep.tile([P, 2, toks, NODES], F32)
         nc.scalar.activation(out=gates[:, 0], in_=gate_in[:], func=ACT.Sigmoid)
         nc.scalar.activation(out=gates[:, 1], in_=gate_in[:], func=ACT.Sigmoid, scale=-1.0)
@@ -170,9 +173,13 @@ def tile_fastfeedforwardnetwork_pa_t_kernel(tc, x, node_logits, node_b, w1, b1, 
             tiles = CHUNK_TILES[c]
             i0 = FIRST_TILE[c]
             spread = spread_pool.tile([P, tiles, LEAVES, REPEAT], F32)
-            nc.vector.tensor_copy(
+            nc.gpsimd.tensor_scalar(
                 out=spread[:],
-                in_=probs[:, i0 : i0 + tiles, :].unsqueeze(3).to_broadcast([P, tiles, LEAVES, REPEAT]),
+                in0=probs[:, i0 : i0 + tiles, :].unsqueeze(3).to_broadcast([P, tiles, LEAVES, REPEAT]),
+                scalar1=1.0,
+                scalar2=0.0,
+                op0=ALU.mult,
+                op1=ALU.add,
             )
             spread_tiles[c] = spread
 
@@ -294,7 +301,7 @@ def tile_fastfeedforwardnetwork_pa_t_kernel(tc, x, node_logits, node_b, w1, b1, 
                     start=True,
                     stop=True,
                 )
-                if half == 1 and ((FIRST_TILE[c] + j) % TILES == VECTOR_TILE or c >= CHUNKS - 2):
+                if half == 1 and ((FIRST_TILE[c] + j) % TILES in VSHARE or FIRST_TILE[c] + j >= VFROM):
                     nc.vector.tensor_copy(out=result[:, e0 : e0 + BANK], in_=o[:])
                 else:
                     nc.scalar.copy(out=result[:, e0 : e0 + BANK], in_=o[:])
@@ -305,13 +312,12 @@ def tile_fastfeedforwardnetwork_pa_t_kernel(tc, x, node_logits, node_b, w1, b1, 
 
         for g in range(PASSES):
             transpose_x(0, g)
-        for c in range(2):
+        for c in range(CHUNKS):
             spread_probs(c)
-            turn_probs(c)
+            if c < SPREAD_HEAD:
+                turn_probs(c)
         for g in range(PASSES):
             quantise_x(0, g)
-        spread_probs(2)
-        turn_probs(2)
         for s in range(PACK):
             regroup_w1(nc.vector.tensor_copy, 0, s)
         quantise_w1(0, 0, PACK)
@@ -320,20 +326,14 @@ def tile_fastfeedforwardnetwork_pa_t_kernel(tc, x, node_logits, node_b, w1, b1, 
         for s in range(2):
             regroup_w1(nc.vector.tensor_copy, 1, s)
             quantise_w1(1, s, s + 1)
-        for g in range(PASSES):
-            transpose_x(1, g)
+        b1_col = keep.tile([P, PACK], F32)
+        nc.vector.tensor_copy(out=b1_col[:], in_=b1_bf[:])
 
-        x_due = [(2, 2, 0), (3, 2, 1)] + [
-            (FIRST_TILE[c] - X_LEAD[g if CHUNK_TILES[c] == TILES else 1], c, g)
-            for c in range(3, CHUNKS)
-            for g in range(PASSES)
-        ]
+        x_due = [(X_DUE(k), c, g) for k, (c, g) in enumerate((c, g) for c in range(1, CHUNKS) for g in range(PASSES))]
         out_due = [
             (FIRST_TILE[c] + CHUNK_TILES[c] + OUT_LAG + j, c, j) for c in range(CHUNKS) for j in range(CHUNK_TILES[c])
         ]
-        to_quantise = [(1, 0), (1, 1)]
-        to_spread = list(range(3, CHUNKS))
-        to_turn = []
+        to_quantise = []
         to_load = list(range(X_BUFS, ROUNDS))
         for c in range(CHUNKS):
             for s in range(PACK):
@@ -341,31 +341,27 @@ def tile_fastfeedforwardnetwork_pa_t_kernel(tc, x, node_logits, node_b, w1, b1, 
                 hidden_sums(c, s)
                 if c == 0 and s in (0, 1):
                     quantise_w1(1, s + 2, s + 3)
+                if c == 0:
+                    for cc in range(SPREAD_HEAD + s * SPREAD_STEP, min(SPREAD_HEAD + s * SPREAD_STEP + SPREAD_STEP, CHUNKS)):
+                        turn_probs(cc)
                 while to_quantise:
                     quantise_x(*to_quantise.pop(0))
-                if c == 0 and s == 2:
+                if c == 0 and s == W2_STEP:
                     regroup_w2()
-                if c == 0 and s == 3:
+                if c == 0 and s == W2_STEP + 1:
                     quantise_w2(0, BANK)
-                if c == 1 and s == 0:
                     quantise_w2(BANK, D)
                 while out_due and out_due[0][0] <= clock:
                     output_tile(*out_due.pop(0)[1:])
                 if s == PACK - 1:
                     relu_hidden(c)
-                if x_due and x_due[0][0] <= clock:
-                    if to_turn:
-                        turn_probs(to_turn.pop(0))
-                    while x_due and x_due[0][0] <= clock:
-                        due, xc, g = x_due.pop(0)
-                        transpose_x(xc, g)
-                        to_quantise.append((xc, g))
-                        if g == PASSES - 1 and CHUNK_TILES[xc] == TILES and to_load:
-                            load_x(to_load.pop(0))
+                while x_due and x_due[0][0] <= clock:
+                    due, xc, g = x_due.pop(0)
+                    transpose_x(xc, g)
+                    to_quantise.append((xc, g))
+                    if g == PASSES - 1 and xc < CHUNKS - 1 and to_load:
+                        load_x(to_load.pop(0))
                 if s == PACK - 1:
                     quantise_hidden(c)
-                if to_spread and not to_turn:
-                    to_turn.append(to_spread[0])
-                    spread_probs(to_spread.pop(0))
         for due, c, j in out_due:
             output_tile(c, j)

@@ -31,7 +31,9 @@ CHUNK_TILES = (4, 4, 4, 4, 4, 4, 4, 2, 2)
 CHUNKS = len(CHUNK_TILES)
 FIRST_TILE = tuple(sum(CHUNK_TILES[:c]) for c in range(CHUNKS))
 OUT_LAG = 2
-X_DUE = lambda k: k if k < 6 else 2 * k - 5
+X_DUE = lambda k: 4 * (k // 2) + X0 + 1
+X0 = 2
+X1 = 2
 W2_STEP = 2
 SPREAD_HEAD = 5
 SPREAD_STEP = 1
@@ -78,6 +80,7 @@ def tile_fastfeedforwardnetwork_pa_t_kernel(tc, x, node_logits, node_b, w1, b1, 
 
         load_x(0, 0, TILES // 2)
         load_x(0, TILES // 2, TILES)
+        load_x(1)
         w1_raw = keep.tile([P, PASSES, LEAVES, PACK, HIDDEN // PACK, PACK], BF16)
         for g in range(PASSES):
             nc.sync.dma_start(
@@ -86,7 +89,6 @@ def tile_fastfeedforwardnetwork_pa_t_kernel(tc, x, node_logits, node_b, w1, b1, 
             )
         b1_bf = keep.tile([P, PACK], BF16)
         nc.sync.dma_start(out=b1_bf[:], in_=b1.rearrange("l (f s) -> (l f) s", s=PACK))
-        load_x(1)
         w2_raw = keep.tile([P, PACK, D], BF16)
         nc.sync.dma_start(
             out=w2_raw[:].rearrange("p s e -> p (s e)"),
@@ -173,13 +175,9 @@ def tile_fastfeedforwardnetwork_pa_t_kernel(tc, x, node_logits, node_b, w1, b1, 
             tiles = CHUNK_TILES[c]
             i0 = FIRST_TILE[c]
             spread = spread_pool.tile([P, tiles, LEAVES, REPEAT], F32)
-            nc.gpsimd.tensor_scalar(
+            nc.vector.tensor_copy(
                 out=spread[:],
-                in0=probs[:, i0 : i0 + tiles, :].unsqueeze(3).to_broadcast([P, tiles, LEAVES, REPEAT]),
-                scalar1=1.0,
-                scalar2=0.0,
-                op0=ALU.mult,
-                op1=ALU.add,
+                in_=probs[:, i0 : i0 + tiles, :].unsqueeze(3).to_broadcast([P, tiles, LEAVES, REPEAT]),
             )
             spread_tiles[c] = spread
 
@@ -214,18 +212,11 @@ def tile_fastfeedforwardnetwork_pa_t_kernel(tc, x, node_logits, node_b, w1, b1, 
             )
 
         def regroup_w2():
-            nc.vector.tensor_copy(
-                out=w2_grouped[:, 0:BANK, :].rearrange("p (c i) s -> p c s i", i=RUN),
-                in_=w2_raw[:, :, 0:BANK].rearrange("p s (c i) -> p c s i", i=RUN),
-            )
-            nc.gpsimd.tensor_scalar(
-                out=w2_grouped[:, BANK:D, :],
-                in0=w2_raw[:, :, BANK:D].rearrange("p s e -> p e s"),
-                scalar1=1.0,
-                scalar2=0.0,
-                op0=ALU.mult,
-                op1=ALU.add,
-            )
+            for copy, e0 in ((nc.vector.tensor_copy, 0), (nc.scalar.copy, BANK)):
+                copy(
+                    out=w2_grouped[:, e0 : e0 + BANK, :].rearrange("p (c i) s -> p c s i", i=RUN),
+                    in_=w2_raw[:, :, e0 : e0 + BANK].rearrange("p s (c i) -> p c s i", i=RUN),
+                )
 
         def quantise_w2(e0, e1):
             nc.vector.quantize_mx(
@@ -318,6 +309,8 @@ def tile_fastfeedforwardnetwork_pa_t_kernel(tc, x, node_logits, node_b, w1, b1, 
                 turn_probs(c)
         for g in range(PASSES):
             quantise_x(0, g)
+        for g in range(PASSES):
+            transpose_x(1, g)
         for s in range(PACK):
             regroup_w1(nc.vector.tensor_copy, 0, s)
         quantise_w1(0, 0, PACK)
@@ -326,10 +319,12 @@ def tile_fastfeedforwardnetwork_pa_t_kernel(tc, x, node_logits, node_b, w1, b1, 
         for s in range(2):
             regroup_w1(nc.vector.tensor_copy, 1, s)
             quantise_w1(1, s, s + 1)
+        for g in range(PASSES):
+            quantise_x(1, g)
         b1_col = keep.tile([P, PACK], F32)
         nc.vector.tensor_copy(out=b1_col[:], in_=b1_bf[:])
 
-        x_due = [(X_DUE(k), c, g) for k, (c, g) in enumerate((c, g) for c in range(1, CHUNKS) for g in range(PASSES))]
+        x_due = [(X_DUE(k), c, g) for k, (c, g) in enumerate((c, g) for c in range(2, CHUNKS) for g in range(PASSES))]
         out_due = [
             (FIRST_TILE[c] + CHUNK_TILES[c] + OUT_LAG + j, c, j) for c in range(CHUNKS) for j in range(CHUNK_TILES[c])
         ]

@@ -46,8 +46,8 @@ FLOPS = 2 * TOKENS * D * LF * 2
 
 def tile_fastfeedforwardnetwork_pa_t_kernel(tc, x, node_logits, node_b, w1, b1, w2, out):
     nc = tc.nc
-    x_rounds = x.flatten_outer_dims().rearrange("(r p j) d -> r p j d", p=P, j=TILES)
-    out_rounds = out.flatten_outer_dims().rearrange("(r p j) e -> r p j e", p=P, j=TILES)
+    x_rounds = x.flatten_outer_dims().rearrange("(p r j) d -> r p j d", p=P, j=TILES)
+    out_rounds = out.flatten_outer_dims().rearrange("(p r j) e -> r p j e", p=P, j=TILES)
 
     with ExitStack() as ctx:
         keep = ctx.enter_context(tc.tile_pool(name="keep", bufs=1))
@@ -63,12 +63,10 @@ def tile_fastfeedforwardnetwork_pa_t_kernel(tc, x, node_logits, node_b, w1, b1, 
 
         toks = TOKENS // P
         logits = keep.tile([P, toks, NODES], BF16)
-        nc.sync.dma_start(
-            out=logits[:].rearrange("p (r j) n -> p r (j n)", j=TILES),
-            in_=node_logits.flatten_outer_dims().rearrange("(r p j) n -> p r (j n)", p=P, j=TILES),
-        )
-        node_bias = keep.tile([P, NODES], BF16)
-        nc.sync.dma_start(out=node_bias[:], in_=node_b.partition_broadcast(P))
+        nc.sync.dma_start(out=logits[:], in_=node_logits.flatten_outer_dims().rearrange("(p i) n -> p i n", p=P))
+        bias_rows = keep.tile([P, NODES], BF16)
+        nc.gpsimd.memset(bias_rows[:], 0.0)
+        nc.sync.dma_start(out=bias_rows[0:1, :], in_=node_b.unsqueeze(0))
 
         x_tiles = {}
 
@@ -97,6 +95,9 @@ def tile_fastfeedforwardnetwork_pa_t_kernel(tc, x, node_logits, node_b, w1, b1, 
         for r in range(2, X_BUFS):
             load_x(r)
 
+        ones = keep.tile([P, P], BF16)
+        nc.gpsimd.memset(ones[:], 1.0)
+
         warm = keep.tile([P, 1], F32)
         nc.gpsimd.memset(warm[:], 0.0)
         nc.scalar.activation(out=warm[:], in_=warm[:], func=ACT.Sigmoid)
@@ -104,6 +105,8 @@ def tile_fastfeedforwardnetwork_pa_t_kernel(tc, x, node_logits, node_b, w1, b1, 
         ident = keep.tile([P, P], F32)
         make_identity(nc, ident[:])
 
+        node_bias = turn_psum.tile([P, NODES], F32, tag="turn")
+        nc.tensor.matmul(node_bias[:], lhsT=ones[:], rhs=bias_rows[:], start=True, stop=True)
         gate_in = keep.tile([P, toks, NODES], F32)
         nc.vector.tensor_tensor(
             out=gate_in[:],

@@ -37,7 +37,7 @@ X1 = 2
 W2_STEP = 2
 SPREAD_HEAD = 5
 SPREAD_STEP = 1
-VSHARE = (1,)
+VSHARE = ()
 VFROM = 28
 RUN = 4
 

@@ -22,26 +22,29 @@ HIDDEN = 32
 LF = LEAVES * HIDDEN
 PASSES = D // (P * PACK)
 BANK = 512
-REPEAT = P // LEAVES
-X_BUFS = 6
 ROUND = 512
 ROUNDS = TOKENS // ROUND
 TILES = ROUND // P
-CHUNK_TILES = (4, 4, 4, 4, 4, 4, 4, 2, 2)
-CHUNKS = len(CHUNK_TILES)
-FIRST_TILE = tuple(sum(CHUNK_TILES[:c]) for c in range(CHUNKS))
-OUT_LAG = 2
-X_DUE = lambda k: 4 * (k // 2) + X0 + 1
-X0 = 2
-X1 = 2
-W2_STEP = 2
-SPREAD_HEAD = 5
-SPREAD_STEP = 1
-VSHARE = ()
-VFROM = 28
+REPEAT = P // LEAVES
+X_BUFS = 6
+STEPS = ROUNDS * PACK
+OUT_LAG = 6
+HEAD_ROUNDS = 2
+HEAD_LEAVES = 6
+W1_VECTOR = 2
+W2_REGROUP_STEP = 1
+W2_QUANTISE_STEP = 2
 RUN = 4
 
 FLOPS = 2 * TOKENS * D * LF * 2
+
+
+def transpose_step(r):
+    if r == HEAD_ROUNDS:
+        return PACK - 1
+    if r == HEAD_ROUNDS + 1:
+        return PACK
+    return PACK * (r - 2) - 1
 
 
 def tile_fastfeedforwardnetwork_pa_t_kernel(tc, x, node_logits, node_b, w1, b1, w2, out):
@@ -54,7 +57,7 @@ def tile_fastfeedforwardnetwork_pa_t_kernel(tc, x, node_logits, node_b, w1, b1, 
         x_pool = ctx.enter_context(tc.tile_pool(name="x_pool", bufs=X_BUFS))
         xg_pool = ctx.enter_context(tc.tile_pool(name="xg_pool", bufs=2))
         xq_pool = ctx.enter_context(tc.tile_pool(name="xq_pool", bufs=4))
-        spread_pool = ctx.enter_context(tc.tile_pool(name="spread_pool", bufs=8))
+        spread_pool = ctx.enter_context(tc.tile_pool(name="spread_pool", bufs=ROUNDS))
         h_pool = ctx.enter_context(tc.tile_pool(name="h_pool", bufs=2))
         out_pool = ctx.enter_context(tc.tile_pool(name="out_pool", bufs=8))
         a_psum = ctx.enter_context(tc.psum_pool(name="a_psum", bufs=3))
@@ -67,6 +70,9 @@ def tile_fastfeedforwardnetwork_pa_t_kernel(tc, x, node_logits, node_b, w1, b1, 
         bias_rows = keep.tile([P, NODES], BF16)
         nc.gpsimd.memset(bias_rows[:], 0.0)
         nc.sync.dma_start(out=bias_rows[0:1, :], in_=node_b.unsqueeze(0))
+        b1_rows = keep.tile([P, LF], BF16)
+        nc.vector.memset(b1_rows[:], 0.0)
+        nc.sync.dma_start(out=b1_rows[0:1, :], in_=b1.rearrange("(o l) f -> o (l f)", o=1))
 
         x_tiles = {}
 
@@ -85,14 +91,12 @@ def tile_fastfeedforwardnetwork_pa_t_kernel(tc, x, node_logits, node_b, w1, b1, 
                 out=w1_raw[:, g].rearrange("p l t f s -> p l (t f s)"),
                 in_=w1[:, g * P * PACK : (g + 1) * P * PACK, :].rearrange("l (p t) f -> p l (t f)", p=P, t=PACK),
             )
-        b1_bf = keep.tile([P, PACK], BF16)
-        nc.sync.dma_start(out=b1_bf[:], in_=b1.rearrange("l (f s) -> (l f) s", s=PACK))
         w2_raw = keep.tile([P, PACK, D], BF16)
         nc.sync.dma_start(
             out=w2_raw[:].rearrange("p s e -> p (s e)"),
             in_=w2.rearrange("l (f s) e -> (l f) (s e)", s=PACK),
         )
-        for r in range(2, X_BUFS):
+        for r in range(HEAD_ROUNDS, X_BUFS):
             load_x(r)
 
         ones = keep.tile([P, P], BF16)
@@ -107,6 +111,12 @@ def tile_fastfeedforwardnetwork_pa_t_kernel(tc, x, node_logits, node_b, w1, b1, 
 
         node_bias = turn_psum.tile([P, NODES], F32, tag="turn")
         nc.tensor.matmul(node_bias[:], lhsT=ones[:], rhs=bias_rows[:], start=True, stop=True)
+        b1_spread = turn_psum.tile([P, PACK], F32, tag="turn")
+        for s in range(PACK):
+            nc.tensor.matmul(
+                b1_spread[:, s : s + 1], lhsT=b1_rows[:, s::PACK], rhs=ones[:, 0:1], start=True, stop=True
+            )
+
         gate_in = keep.tile([P, toks, NODES], F32)
         nc.vector.tensor_tensor(
             out=gate_in[:],
@@ -114,6 +124,8 @@ def tile_fastfeedforwardnetwork_pa_t_kernel(tc, x, node_logits, node_b, w1, b1, 
             in1=node_bias[:].unsqueeze(1).to_broadcast([P, toks, NODES]),
             op=ALU.add,
         )
+        b1_col = keep.tile([P, PACK], F32)
+        nc.vector.tensor_copy(out=b1_col[:], in_=b1_spread[:])
         gates = keep.tile([P, 2, toks, NODES], F32)
         nc.scalar.activation(out=gates[:, 0], in_=gate_in[:], func=ACT.Sigmoid)
         nc.scalar.activation(out=gates[:, 1], in_=gate_in[:], func=ACT.Sigmoid, scale=-1.0)
@@ -134,65 +146,56 @@ def tile_fastfeedforwardnetwork_pa_t_kernel(tc, x, node_logits, node_b, w1, b1, 
         xg_tiles = {}
         xq_tiles = {}
 
-        def transpose_x(c, g):
-            tiles = CHUNK_TILES[c]
-            if g == 0:
-                x_grouped = xg_pool.tile([P, PASSES, tiles * P, PACK], BF16, align_bytes=64)
-                x_codes = xq_pool.tile([P, PASSES, tiles * P], U32, align_bytes=64)
-                x_scales = xq_pool.tile([P, PASSES, tiles * P], U8, align_bytes=64)
-                xg_tiles[c] = x_grouped
-                xq_tiles[c] = (x_codes, x_scales)
-            r, j0 = divmod(FIRST_TILE[c], TILES)
+        def transpose_x(r):
+            x_grouped = xg_pool.tile([P, PASSES, ROUND, PACK], BF16, align_bytes=64)
+            x_codes = xq_pool.tile([P, PASSES, ROUND], U32, align_bytes=64)
+            x_scales = xq_pool.tile([P, PASSES, ROUND], U8, align_bytes=64)
+            xg_tiles[r] = x_grouped
+            xq_tiles[r] = (x_codes, x_scales)
             x_words = x_tiles[r][:].bitcast(F32)
-            grouped_words = xg_tiles[c][:].bitcast(F32)
-            for half in range(tiles // 2):
-                xt = turn_psum.tile([P, 2, 2 * P], F32, tag="turn")
-                for u in range(2):
-                    for jj in range(2):
-                        nc.tensor.transpose(
-                            xt[:, u, jj * P : (jj + 1) * P],
-                            x_words[:, j0 + 2 * half + jj, 2 * P * g + u : 2 * P * (g + 1) : 2],
-                            ident[:],
-                        )
-                nc.scalar.copy(
-                    out=grouped_words[:, g, half * 2 * P : (half + 1) * 2 * P, :],
-                    in_=xt[:].rearrange("p u w -> p w u"),
+            grouped_words = x_grouped[:].bitcast(F32)
+            for g in range(PASSES):
+                for half in range(TILES // 2):
+                    xt = turn_psum.tile([P, 2, 2 * P], F32, tag="turn")
+                    for u in range(2):
+                        for jj in range(2):
+                            nc.tensor.transpose(
+                                xt[:, u, jj * P : (jj + 1) * P],
+                                x_words[:, 2 * half + jj, 2 * P * g + u : 2 * P * (g + 1) : 2],
+                                ident[:],
+                            )
+                    nc.scalar.copy(
+                        out=grouped_words[:, g, half * 2 * P : (half + 1) * 2 * P, :],
+                        in_=xt[:].rearrange("p u w -> p w u"),
+                    )
+
+        def quantise_x(r):
+            x_codes, x_scales = xq_tiles[r]
+            for g in range(PASSES):
+                nc.vector.quantize_mx(
+                    out=x_codes[:, g, :].bitcast(FP8X4),
+                    scales=x_scales[:, g, :],
+                    in_=xg_tiles[r][:, g].rearrange("p w t -> p (w t)"),
                 )
 
-        def quantise_x(c, g):
-            x_codes, x_scales = xq_tiles[c]
-            nc.vector.quantize_mx(
-                out=x_codes[:, g, :].bitcast(FP8X4),
-                scales=x_scales[:, g, :],
-                in_=xg_tiles[c][:, g].rearrange("p w t -> p (w t)"),
-            )
-
-        leaf_rows = keep.tile([P, TOKENS], F32)
-
-        def columns_of(c):
-            return slice(FIRST_TILE[c] * P, (FIRST_TILE[c] + CHUNK_TILES[c]) * P)
-
+        leaf_rows = keep.tile([P, ROUNDS, ROUND], F32)
         spread_tiles = {}
 
-        def spread_probs(c):
-            tiles = CHUNK_TILES[c]
-            i0 = FIRST_TILE[c]
-            spread = spread_pool.tile([P, tiles, LEAVES, REPEAT], F32)
+        def spread_probs(r):
+            spread = spread_pool.tile([P, TILES, LEAVES, REPEAT], F32)
             nc.vector.tensor_copy(
                 out=spread[:],
-                in_=probs[:, i0 : i0 + tiles, :].unsqueeze(3).to_broadcast([P, tiles, LEAVES, REPEAT]),
+                in_=probs[:, r * TILES : (r + 1) * TILES, :].unsqueeze(3).to_broadcast([P, TILES, LEAVES, REPEAT]),
             )
-            spread_tiles[c] = spread
+            spread_tiles[r] = spread
 
-        def turn_probs(c):
-            tiles = CHUNK_TILES[c]
-            spread = spread_tiles[c]
-            rows = turn_psum.tile([P, tiles * P], F32, tag="turn")
-            for j in range(tiles):
+        def turn_probs(r):
+            rows = turn_psum.tile([P, ROUND], F32, tag="turn")
+            for j in range(TILES):
                 nc.tensor.transpose(
-                    rows[:, j * P : (j + 1) * P], spread[:, j].rearrange("p l c -> p (l c)"), ident[:]
+                    rows[:, j * P : (j + 1) * P], spread_tiles[r][:, j].rearrange("p l c -> p (l c)"), ident[:]
                 )
-            nc.scalar.copy(out=leaf_rows[:, columns_of(c)], in_=rows[:])
+            nc.scalar.copy(out=leaf_rows[:, r, :], in_=rows[:])
 
         w1_grouped = keep.tile([P, PASSES, PACK, P, PACK], BF16, align_bytes=64)
         w1_codes = keep.tile([P, PASSES, PACK, P], U32, align_bytes=64)
@@ -221,24 +224,24 @@ def tile_fastfeedforwardnetwork_pa_t_kernel(tc, x, node_logits, node_b, w1, b1, 
                     in_=w2_raw[:, :, e0 : e0 + BANK].rearrange("p s (c i) -> p c s i", i=RUN),
                 )
 
-        def quantise_w2(e0, e1):
-            nc.vector.quantize_mx(
-                out=w2_codes[:, e0:e1].bitcast(FP8X4),
-                scales=w2_scales[:, e0:e1],
-                in_=w2_grouped[:, e0:e1].rearrange("p e s -> p (e s)"),
-            )
+        def quantise_w2():
+            for e0 in range(0, D, BANK):
+                nc.vector.quantize_mx(
+                    out=w2_codes[:, e0 : e0 + BANK].bitcast(FP8X4),
+                    scales=w2_scales[:, e0 : e0 + BANK],
+                    in_=w2_grouped[:, e0 : e0 + BANK].rearrange("p e s -> p (e s)"),
+                )
 
         weighted_tiles = {}
         h_grouped_tiles = {}
         hq_tiles = {}
 
-        def hidden_sums(c, s):
-            tokens = CHUNK_TILES[c] * P
+        def hidden_sums(r, s):
             if s == 0:
-                weighted = h_pool.tile([P, PACK, tokens], BF16)
-                weighted_tiles[c] = weighted
-            x_codes, x_scales = xq_tiles[c]
-            a = a_psum.tile([P, tokens], F32)
+                weighted = h_pool.tile([P, PACK, ROUND], BF16)
+                weighted_tiles[r] = weighted
+            x_codes, x_scales = xq_tiles[r]
+            a = a_psum.tile([P, ROUND], F32)
             for g in range(PASSES):
                 nc.tensor.matmul_mx(
                     out=a[:],
@@ -250,38 +253,37 @@ def tile_fastfeedforwardnetwork_pa_t_kernel(tc, x, node_logits, node_b, w1, b1, 
                     stop=(g == PASSES - 1),
                 )
             nc.vector.scalar_tensor_tensor(
-                out=weighted_tiles[c][:, s, :],
+                out=weighted_tiles[r][:, s, :],
                 in0=a[:],
                 scalar=b1_col[:, s : s + 1],
-                in1=leaf_rows[:, columns_of(c)],
+                in1=leaf_rows[:, r, :],
                 op0=ALU.add,
                 op1=ALU.mult,
             )
 
-        def relu_hidden(c):
-            h_grouped = h_pool.tile([P, CHUNK_TILES[c] * P, PACK], BF16, align_bytes=64)
+        def relu_hidden(r):
+            h_grouped = h_pool.tile([P, ROUND, PACK], BF16, align_bytes=64)
             nc.vector.tensor_scalar(
                 out=h_grouped[:].rearrange("p (c i) s -> p c s i", i=RUN),
-                in0=weighted_tiles[c][:].rearrange("p s (c i) -> p c s i", i=RUN),
+                in0=weighted_tiles[r][:].rearrange("p s (c i) -> p c s i", i=RUN),
                 scalar1=0.0,
                 scalar2=None,
                 op0=ALU.max,
             )
-            h_grouped_tiles[c] = h_grouped
+            h_grouped_tiles[r] = h_grouped
 
-        def quantise_hidden(c):
-            tokens = CHUNK_TILES[c] * P
-            h_codes = h_pool.tile([P, tokens], U32, align_bytes=64)
-            h_scales = h_pool.tile([P, tokens], U8, align_bytes=64)
+        def quantise_hidden(r):
+            h_codes = h_pool.tile([P, ROUND], U32, align_bytes=64)
+            h_scales = h_pool.tile([P, ROUND], U8, align_bytes=64)
             nc.vector.quantize_mx(
                 out=h_codes[:].bitcast(FP8X4),
                 scales=h_scales[:],
-                in_=h_grouped_tiles[c][:].rearrange("p w s -> p (w s)"),
+                in_=h_grouped_tiles[r][:].rearrange("p w s -> p (w s)"),
             )
-            hq_tiles[c] = (h_codes, h_scales)
+            hq_tiles[r] = (h_codes, h_scales)
 
-        def output_tile(c, j):
-            h_codes, h_scales = hq_tiles[c]
+        def output_tile(r, j):
+            h_codes, h_scales = hq_tiles[r]
             result = out_pool.tile([P, D], F32)
             for half in range(D // BANK):
                 e0 = half * BANK
@@ -295,71 +297,51 @@ def tile_fastfeedforwardnetwork_pa_t_kernel(tc, x, node_logits, node_b, w1, b1, 
                     start=True,
                     stop=True,
                 )
-                if half == 1 and ((FIRST_TILE[c] + j) % TILES in VSHARE or FIRST_TILE[c] + j >= VFROM):
+                if r == ROUNDS - 1 and half == 1:
                     nc.vector.tensor_copy(out=result[:, e0 : e0 + BANK], in_=o[:])
                 else:
                     nc.scalar.copy(out=result[:, e0 : e0 + BANK], in_=o[:])
-            nc.sync.dma_start(
-                out=out_rounds[(FIRST_TILE[c] + j) // TILES][:, (FIRST_TILE[c] + j) % TILES, :],
-                in_=result[:],
-            )
+            nc.sync.dma_start(out=out_rounds[r][:, j, :], in_=result[:])
 
-        for g in range(PASSES):
-            transpose_x(0, g)
-        for c in range(CHUNKS):
-            spread_probs(c)
-            if c < SPREAD_HEAD:
-                turn_probs(c)
-        for g in range(PASSES):
-            quantise_x(0, g)
-        for g in range(PASSES):
-            transpose_x(1, g)
+        transpose_x(0)
+        for r in range(ROUNDS):
+            spread_probs(r)
+            if r < HEAD_LEAVES:
+                turn_probs(r)
+        quantise_x(0)
+        transpose_x(1)
         for s in range(PACK):
             regroup_w1(nc.vector.tensor_copy, 0, s)
         quantise_w1(0, 0, PACK)
-        for s in range(2, PACK):
-            regroup_w1(nc.scalar.copy, 1, s)
-        for s in range(2):
-            regroup_w1(nc.vector.tensor_copy, 1, s)
-            quantise_w1(1, s, s + 1)
-        for g in range(PASSES):
-            quantise_x(1, g)
-        b1_col = keep.tile([P, PACK], F32)
-        nc.vector.tensor_copy(out=b1_col[:], in_=b1_bf[:])
+        for s in range(W1_VECTOR, PACK):
+            regroup_w1(nc.scalar.copy, PASSES - 1, s)
+        for s in range(W1_VECTOR):
+            regroup_w1(nc.vector.tensor_copy, PASSES - 1, s)
+            quantise_w1(PASSES - 1, s, s + 1)
+        quantise_x(1)
 
-        x_due = [(X_DUE(k), c, g) for k, (c, g) in enumerate((c, g) for c in range(2, CHUNKS) for g in range(PASSES))]
-        out_due = [
-            (FIRST_TILE[c] + CHUNK_TILES[c] + OUT_LAG + j, c, j) for c in range(CHUNKS) for j in range(CHUNK_TILES[c])
-        ]
-        to_quantise = []
-        to_load = list(range(X_BUFS, ROUNDS))
-        for c in range(CHUNKS):
-            for s in range(PACK):
-                clock = FIRST_TILE[c] + s * CHUNK_TILES[c] / PACK
-                hidden_sums(c, s)
-                if c == 0 and s in (0, 1):
-                    quantise_w1(1, s + 2, s + 3)
-                if c == 0:
-                    for cc in range(SPREAD_HEAD + s * SPREAD_STEP, min(SPREAD_HEAD + s * SPREAD_STEP + SPREAD_STEP, CHUNKS)):
-                        turn_probs(cc)
-                while to_quantise:
-                    quantise_x(*to_quantise.pop(0))
-                if c == 0 and s == W2_STEP:
-                    regroup_w2()
-                if c == 0 and s == W2_STEP + 1:
-                    quantise_w2(0, BANK)
-                    quantise_w2(BANK, D)
-                while out_due and out_due[0][0] <= clock:
-                    output_tile(*out_due.pop(0)[1:])
-                if s == PACK - 1:
-                    relu_hidden(c)
-                while x_due and x_due[0][0] <= clock:
-                    due, xc, g = x_due.pop(0)
-                    transpose_x(xc, g)
-                    to_quantise.append((xc, g))
-                    if g == PASSES - 1 and xc < CHUNKS - 1 and to_load:
-                        load_x(to_load.pop(0))
-                if s == PACK - 1:
-                    quantise_hidden(c)
-        for due, c, j in out_due:
-            output_tile(c, j)
+        x_at = {transpose_step(r): r for r in range(HEAD_ROUNDS, ROUNDS)}
+        for step in range(STEPS + OUT_LAG):
+            r, s = divmod(step, PACK)
+            if step < STEPS:
+                hidden_sums(r, s)
+            if step + W1_VECTOR < PACK:
+                quantise_w1(PASSES - 1, step + W1_VECTOR, step + W1_VECTOR + 1)
+            if step < ROUNDS - HEAD_LEAVES:
+                turn_probs(HEAD_LEAVES + step)
+            if step - 1 in x_at:
+                quantise_x(x_at[step - 1])
+            if step == W2_REGROUP_STEP:
+                regroup_w2()
+            if step == W2_QUANTISE_STEP:
+                quantise_w2()
+            if step >= OUT_LAG:
+                output_tile(*divmod(step - OUT_LAG, TILES))
+            if step < STEPS and s == PACK - 1:
+                relu_hidden(r)
+            if step in x_at:
+                transpose_x(x_at[step])
+                if x_at[step] + X_BUFS - HEAD_ROUNDS < ROUNDS:
+                    load_x(x_at[step] + X_BUFS - HEAD_ROUNDS)
+            if step < STEPS and s == PACK - 1:
+                quantise_hidden(r)

from contextlib import ExitStack

import concourse.mybir as mybir
from concourse.masks import make_identity

F32 = mybir.dt.float32
BF16 = mybir.dt.bfloat16
U32 = mybir.dt.uint32
U8 = mybir.dt.uint8
FP8X4 = mybir.dt.float8_e4m3fn_x4
ALU = mybir.AluOpType
ACT = mybir.ActivationFunctionType

P = 128
PACK = 4
TOKENS = 4096
D = 1024
DEPTH = 4
LEAVES = 16
NODES = 15
HIDDEN = 32
LF = LEAVES * HIDDEN
PASSES = D // (P * PACK)
BANK = 512
ROUND = 512
ROUNDS = TOKENS // ROUND
TILES = ROUND // P
REPEAT = P // LEAVES
X_BUFS = 6
STEPS = ROUNDS * PACK
OUT_LAG = 6
HEAD_ROUNDS = 2
HEAD_LEAVES = 6
W1_VECTOR = 2
W2_REGROUP_STEP = 1
W2_QUANTISE_STEP = 2
RUN = 4

FLOPS = 2 * TOKENS * D * LF * 2


def transpose_step(r):
    if r == HEAD_ROUNDS:
        return PACK - 1
    if r == HEAD_ROUNDS + 1:
        return PACK
    return PACK * (r - 2) - 1


def tile_fastfeedforwardnetwork_pa_t_kernel(tc, x, node_logits, node_b, w1, b1, w2, out):
    nc = tc.nc
    x_rounds = x.flatten_outer_dims().rearrange("(p r j) d -> r p j d", p=P, j=TILES)
    out_rounds = out.flatten_outer_dims().rearrange("(p r j) e -> r p j e", p=P, j=TILES)

    with ExitStack() as ctx:
        keep = ctx.enter_context(tc.tile_pool(name="keep", bufs=1))
        x_pool = ctx.enter_context(tc.tile_pool(name="x_pool", bufs=X_BUFS))
        xg_pool = ctx.enter_context(tc.tile_pool(name="xg_pool", bufs=2))
        xq_pool = ctx.enter_context(tc.tile_pool(name="xq_pool", bufs=4))
        spread_pool = ctx.enter_context(tc.tile_pool(name="spread_pool", bufs=ROUNDS))
        h_pool = ctx.enter_context(tc.tile_pool(name="h_pool", bufs=2))
        out_pool = ctx.enter_context(tc.tile_pool(name="out_pool", bufs=8))
        a_psum = ctx.enter_context(tc.psum_pool(name="a_psum", bufs=3))
        turn_psum = ctx.enter_context(tc.psum_pool(name="turn_psum", bufs=5))
        ctx.enter_context(tc.manual_schedule())

        toks = TOKENS // P
        logits = keep.tile([P, toks, NODES], BF16)
        nc.sync.dma_start(out=logits[:], in_=node_logits.flatten_outer_dims().rearrange("(p i) n -> p i n", p=P))
        bias_rows = keep.tile([P, NODES], BF16)
        nc.gpsimd.memset(bias_rows[:], 0.0)
        nc.sync.dma_start(out=bias_rows[0:1, :], in_=node_b.unsqueeze(0))
        b1_rows = keep.tile([P, LF], BF16)
        nc.vector.memset(b1_rows[:], 0.0)
        nc.sync.dma_start(out=b1_rows[0:1, :], in_=b1.rearrange("(o l) f -> o (l f)", o=1))

        x_tiles = {}

        def load_x(r, j0=0, j1=TILES):
            if j0 == 0:
                x_raw = x_pool.tile([P, TILES, D], BF16)
                x_tiles[r] = x_raw
            nc.sync.dma_start(out=x_tiles[r][:, j0:j1], in_=x_rounds[r][:, j0:j1])

        load_x(0, 0, TILES // 2)
        load_x(0, TILES // 2, TILES)
        load_x(1)
        w1_raw = keep.tile([P, PASSES, LEAVES, PACK, HIDDEN // PACK, PACK], BF16)
        for g in range(PASSES):
            nc.sync.dma_start(
                out=w1_raw[:, g].rearrange("p l t f s -> p l (t f s)"),
                in_=w1[:, g * P * PACK : (g + 1) * P * PACK, :].rearrange("l (p t) f -> p l (t f)", p=P, t=PACK),
            )
        w2_raw = keep.tile([P, PACK, D], BF16)
        nc.sync.dma_start(
            out=w2_raw[:].rearrange("p s e -> p (s e)"),
            in_=w2.rearrange("l (f s) e -> (l f) (s e)", s=PACK),
        )
        for r in range(HEAD_ROUNDS, X_BUFS):
            load_x(r)

        ones = keep.tile([P, P], BF16)
        nc.gpsimd.memset(ones[:], 1.0)

        warm = keep.tile([P, 1], F32)
        nc.gpsimd.memset(warm[:], 0.0)
        nc.scalar.activation(out=warm[:], in_=warm[:], func=ACT.Sigmoid)

        ident = keep.tile([P, P], F32)
        make_identity(nc, ident[:])

        node_bias = turn_psum.tile([P, NODES], F32, tag="turn")
        nc.tensor.matmul(node_bias[:], lhsT=ones[:], rhs=bias_rows[:], start=True, stop=True)
        b1_spread = turn_psum.tile([P, PACK], F32, tag="turn")
        for s in range(PACK):
            nc.tensor.matmul(
                b1_spread[:, s : s + 1], lhsT=b1_rows[:, s::PACK], rhs=ones[:, 0:1], start=True, stop=True
            )

        gate_in = keep.tile([P, toks, NODES], F32)
        nc.vector.tensor_tensor(
            out=gate_in[:],
            in0=logits[:],
            in1=node_bias[:].unsqueeze(1).to_broadcast([P, toks, NODES]),
            op=ALU.add,
        )
        b1_col = keep.tile([P, PACK], F32)
        nc.vector.tensor_copy(out=b1_col[:], in_=b1_spread[:])
        gates = keep.tile([P, 2, toks, NODES], F32)
        nc.scalar.activation(out=gates[:, 0], in_=gate_in[:], func=ACT.Sigmoid)
        nc.scalar.activation(out=gates[:, 1], in_=gate_in[:], func=ACT.Sigmoid, scale=-1.0)
        sides = gates[:].rearrange("p s i n -> p i n s")
        probs = sides[:, :, 0, :]
        for level in range(1, DEPTH):
            nodes = 2 ** level
            first = nodes - 1
            children = keep.tile([P, toks, nodes, 2], F32, name="children%d" % level)
            nc.vector.tensor_tensor(
                out=children[:],
                in0=probs.unsqueeze(3).to_broadcast([P, toks, nodes, 2]),
                in1=sides[:, :, first : first + nodes, :],
                op=ALU.mult,
            )
            probs = children[:].rearrange("p i n s -> p i (n s)")

        xg_tiles = {}
        xq_tiles = {}

        def transpose_x(r):
            x_grouped = xg_pool.tile([P, PASSES, ROUND, PACK], BF16, align_bytes=64)
            x_codes = xq_pool.tile([P, PASSES, ROUND], U32, align_bytes=64)
            x_scales = xq_pool.tile([P, PASSES, ROUND], U8, align_bytes=64)
            xg_tiles[r] = x_grouped
            xq_tiles[r] = (x_codes, x_scales)
            x_words = x_tiles[r][:].bitcast(F32)
            grouped_words = x_grouped[:].bitcast(F32)
            for g in range(PASSES):
                for half in range(TILES // 2):
                    xt = turn_psum.tile([P, 2, 2 * P], F32, tag="turn")
                    for u in range(2):
                        for jj in range(2):
                            nc.tensor.transpose(
                                xt[:, u, jj * P : (jj + 1) * P],
                                x_words[:, 2 * half + jj, 2 * P * g + u : 2 * P * (g + 1) : 2],
                                ident[:],
                            )
                    nc.scalar.copy(
                        out=grouped_words[:, g, half * 2 * P : (half + 1) * 2 * P, :],
                        in_=xt[:].rearrange("p u w -> p w u"),
                    )

        def quantise_x(r):
            x_codes, x_scales = xq_tiles[r]
            for g in range(PASSES):
                nc.vector.quantize_mx(
                    out=x_codes[:, g, :].bitcast(FP8X4),
                    scales=x_scales[:, g, :],
                    in_=xg_tiles[r][:, g].rearrange("p w t -> p (w t)"),
                )

        leaf_rows = keep.tile([P, ROUNDS, ROUND], F32)
        spread_tiles = {}

        def spread_probs(r):
            spread = spread_pool.tile([P, TILES, LEAVES, REPEAT], F32)
            nc.vector.tensor_copy(
                out=spread[:],
                in_=probs[:, r * TILES : (r + 1) * TILES, :].unsqueeze(3).to_broadcast([P, TILES, LEAVES, REPEAT]),
            )
            spread_tiles[r] = spread

        def turn_probs(r):
            rows = turn_psum.tile([P, ROUND], F32, tag="turn")
            for j in range(TILES):
                nc.tensor.transpose(
                    rows[:, j * P : (j + 1) * P], spread_tiles[r][:, j].rearrange("p l c -> p (l c)"), ident[:]
                )
            nc.scalar.copy(out=leaf_rows[:, r, :], in_=rows[:])

        w1_grouped = keep.tile([P, PASSES, PACK, P, PACK], BF16, align_bytes=64)
        w1_codes = keep.tile([P, PASSES, PACK, P], U32, align_bytes=64)
        w1_scales = keep.tile([P, PASSES, PACK, P], U8, align_bytes=64)
        w2_codes = keep.tile([P, D], U32, align_bytes=64)
        w2_scales = keep.tile([P, D], U8, align_bytes=64)
        w2_grouped = keep.tile([P, D, PACK], BF16, align_bytes=64)

        def regroup_w1(copy, g, s):
            copy(
                out=w1_grouped[:, g, s].rearrange("p (l f) t -> p l f t", l=LEAVES),
                in_=w1_raw[:, g, :, :, :, s].rearrange("p l t f -> p l f t"),
            )

        def quantise_w1(g, s0, s1):
            nc.vector.quantize_mx(
                out=w1_codes[:, g, s0:s1].rearrange("p s m -> p (s m)").bitcast(FP8X4),
                scales=w1_scales[:, g, s0:s1].rearrange("p s m -> p (s m)"),
                in_=w1_grouped[:, g, s0:s1].rearrange("p s m t -> p (s m t)"),
            )

        def regroup_w2():
            for copy, e0 in ((nc.vector.tensor_copy, 0), (nc.scalar.copy, BANK)):
                copy(
                    out=w2_grouped[:, e0 : e0 + BANK, :].rearrange("p (c i) s -> p c s i", i=RUN),
                    in_=w2_raw[:, :, e0 : e0 + BANK].rearrange("p s (c i) -> p c s i", i=RUN),
                )

        def quantise_w2():
            for e0 in range(0, D, BANK):
                nc.vector.quantize_mx(
                    out=w2_codes[:, e0 : e0 + BANK].bitcast(FP8X4),
                    scales=w2_scales[:, e0 : e0 + BANK],
                    in_=w2_grouped[:, e0 : e0 + BANK].rearrange("p e s -> p (e s)"),
                )

        weighted_tiles = {}
        h_grouped_tiles = {}
        hq_tiles = {}

        def hidden_sums(r, s):
            if s == 0:
                weighted = h_pool.tile([P, PACK, ROUND], BF16)
                weighted_tiles[r] = weighted
            x_codes, x_scales = xq_tiles[r]
            a = a_psum.tile([P, ROUND], F32)
            for g in range(PASSES):
                nc.tensor.matmul_mx(
                    out=a[:],
                    lhsT=w1_codes[:, g, s, :].bitcast(FP8X4),
                    lhsT_scale=w1_scales[:, g, s, :],
                    rhs=x_codes[:, g, :].bitcast(FP8X4),
                    rhs_scale=x_scales[:, g, :],
                    start=(g == 0),
                    stop=(g == PASSES - 1),
                )
            nc.vector.scalar_tensor_tensor(
                out=weighted_tiles[r][:, s, :],
                in0=a[:],
                scalar=b1_col[:, s : s + 1],
                in1=leaf_rows[:, r, :],
                op0=ALU.add,
                op1=ALU.mult,
            )

        def relu_hidden(r):
            h_grouped = h_pool.tile([P, ROUND, PACK], BF16, align_bytes=64)
            nc.vector.tensor_scalar(
                out=h_grouped[:].rearrange("p (c i) s -> p c s i", i=RUN),
                in0=weighted_tiles[r][:].rearrange("p s (c i) -> p c s i", i=RUN),
                scalar1=0.0,
                scalar2=None,
                op0=ALU.max,
            )
            h_grouped_tiles[r] = h_grouped

        def quantise_hidden(r):
            h_codes = h_pool.tile([P, ROUND], U32, align_bytes=64)
            h_scales = h_pool.tile([P, ROUND], U8, align_bytes=64)
            nc.vector.quantize_mx(
                out=h_codes[:].bitcast(FP8X4),
                scales=h_scales[:],
                in_=h_grouped_tiles[r][:].rearrange("p w s -> p (w s)"),
            )
            hq_tiles[r] = (h_codes, h_scales)

        def output_tile(r, j):
            h_codes, h_scales = hq_tiles[r]
            result = out_pool.tile([P, D], F32)
            for half in range(D // BANK):
                e0 = half * BANK
                o = turn_psum.tile([P, BANK], F32, tag="turn")
                nc.tensor.matmul_mx(
                    out=o[:],
                    lhsT=h_codes[:, j * P : (j + 1) * P].bitcast(FP8X4),
                    lhsT_scale=h_scales[:, j * P : (j + 1) * P],
                    rhs=w2_codes[:, e0 : e0 + BANK].bitcast(FP8X4),
                    rhs_scale=w2_scales[:, e0 : e0 + BANK],
                    start=True,
                    stop=True,
                )
                if r == ROUNDS - 1 and half == 1:
                    nc.vector.tensor_copy(out=result[:, e0 : e0 + BANK], in_=o[:])
                else:
                    nc.scalar.copy(out=result[:, e0 : e0 + BANK], in_=o[:])
            nc.sync.dma_start(out=out_rounds[r][:, j, :], in_=result[:])

        transpose_x(0)
        for r in range(ROUNDS):
            spread_probs(r)
            if r < HEAD_LEAVES:
                turn_probs(r)
        quantise_x(0)
        transpose_x(1)
        for s in range(PACK):
            regroup_w1(nc.vector.tensor_copy, 0, s)
        quantise_w1(0, 0, PACK)
        for s in range(W1_VECTOR, PACK):
            regroup_w1(nc.scalar.copy, PASSES - 1, s)
        for s in range(W1_VECTOR):
            regroup_w1(nc.vector.tensor_copy, PASSES - 1, s)
            quantise_w1(PASSES - 1, s, s + 1)
        quantise_x(1)

        x_at = {transpose_step(r): r for r in range(HEAD_ROUNDS, ROUNDS)}
        for step in range(STEPS + OUT_LAG):
            r, s = divmod(step, PACK)
            if step < STEPS:
                hidden_sums(r, s)
            if step + W1_VECTOR < PACK:
                quantise_w1(PASSES - 1, step + W1_VECTOR, step + W1_VECTOR + 1)
            if step < ROUNDS - HEAD_LEAVES:
                turn_probs(HEAD_LEAVES + step)
            if step - 1 in x_at:
                quantise_x(x_at[step - 1])
            if step == W2_REGROUP_STEP:
                regroup_w2()
            if step == W2_QUANTISE_STEP:
                quantise_w2()
            if step >= OUT_LAG:
                output_tile(*divmod(step - OUT_LAG, TILES))
            if step < STEPS and s == PACK - 1:
                relu_hidden(r)
            if step in x_at:
                transpose_x(x_at[step])
                if x_at[step] + X_BUFS - HEAD_ROUNDS < ROUNDS:
                    load_x(x_at[step] + X_BUFS - HEAD_ROUNDS)
            if step < STEPS and s == PACK - 1:
                quantise_hidden(r)
